import numpy as np
import ml_dtypes


def mxq(x, axis, fmt="e4m3"):
    dtype, down = {"e4m3": (ml_dtypes.float8_e4m3fn, 7), "e5m2": (ml_dtypes.float8_e5m2, 14)}[fmt]
    v = np.moveaxis(np.asarray(x, np.float32).astype(ml_dtypes.bfloat16).astype(np.float64), axis, -1)
    blocks = v.reshape(v.shape[:-1] + (-1, 32))
    amax = np.abs(blocks).max(-1, keepdims=True)
    byte = np.maximum(np.where(amax > 0, np.frexp(amax)[1] - 1 + 127, 0) - down, 1)
    scale = np.exp2(byte - 127.0)
    codes = (blocks / scale).astype(np.float32).astype(dtype).astype(np.float64)
    return np.moveaxis((codes * scale).reshape(v.shape), -1, axis)


WIDE = False


def mx_kscale(k):
    if not WIDE:
        return np.ones(k)
    levels = np.array([10, -10, 5, -5, 0])
    if k % 512:
        return np.exp2(np.random.permutation(np.resize(levels, k // 32))).repeat(32)
    a = np.empty((k // 512, 16))
    for p in range(k // 512):
        a[p, :8] = np.random.permutation(np.resize(levels, 8))
        for g in range(8):
            far = levels[np.abs(levels - a[p, g]) >= 10]
            a[p, g + 8] = far[np.random.randint(len(far))]
    return np.exp2(a.ravel()).repeat(32)


BF16 = ml_dtypes.bfloat16


def bf(x):
    return np.asarray(x, np.float32).astype(BF16)


def f64(x):
    return np.asarray(x).astype(np.float64)


N, MI0, MI1, MS, MG, MO0, MO1, DV = 128, 512, 256, 1024, 512, 512, 256, 3
EPS = 1e-5


def irlin_mx(x, mul0, mul1, w0, w1):
    n = x.shape[0]
    x0 = x[:, :mul0]
    x1 = x[:, mul0:].reshape(n, mul1, DV).transpose(0, 2, 1)
    y0 = (mxq(x0, 1, "e4m3") @ mxq(w0, 0, "e4m3")) * (1.0 / np.sqrt(mul0))
    y1 = (mxq(x1, 2, "e4m3") @ mxq(w1, 0, "e4m3")).transpose(0, 2, 1) * (1.0 / np.sqrt(mul1))
    return np.concatenate([y0, y1.reshape(n, -1)], axis=-1)


def irlin_plain(x, mul0, mul1, w0, w1):
    n = x.shape[0]
    x0 = x[:, :mul0]
    x1 = x[:, mul0:].reshape(n, mul1, DV).transpose(0, 2, 1)
    y0 = (x0 @ w0) * (1.0 / np.sqrt(mul0))
    y1 = (x1 @ w1).transpose(0, 2, 1) * (1.0 / np.sqrt(mul1))
    return np.concatenate([y0, y1.reshape(n, -1)], axis=-1)


def batchnorm(x, w, b):
    n = x.shape[0]
    s = x[:, :MO0]
    v = x[:, MO0:].reshape(n, MO1, DV)
    s = s - s.mean(0)
    s_inv = 1.0 / np.sqrt((s * s).mean(0) + EPS)
    s = s * (s_inv * w[:MO0]) + b
    v_inv = 1.0 / np.sqrt((v * v).mean(-1).mean(0) + EPS)
    v = v * (v_inv * w[MO0:])[None, :, None]
    return np.concatenate([s, v.reshape(n, -1)], axis=-1)


def setup_inputs():
    s0, s1 = mx_kscale(MS), mx_kscale(MG)
    h0 = (0.1 + 0.3 * np.random.standard_normal((N, MS))) * s0
    h1 = 0.28 * np.random.standard_normal((N, MG, DV)) * s1[None, :, None]
    return {"h2": bf(np.concatenate([h0, h1.reshape(N, -1)], axis=-1)),
            "features": bf(np.random.standard_normal((N, MI0 + DV * MI1))),
            "lin3_W0": bf(np.random.standard_normal((MS, MO0)) / s0[:, None]),
            "lin3_W1": bf(np.random.standard_normal((MG, MO1)) / s1[:, None]),
            "byp_W0": bf(np.random.standard_normal((MI0, MO0))),
            "byp_W1": bf(np.random.standard_normal((MI1, MO1))),
            "bn_weight": bf(1.0 + 0.1 * np.random.standard_normal(MO0 + MO1)),
            "bn_bias": bf(0.1 * np.random.standard_normal(MO0))}


def reference(h2, features, lin3_W0, lin3_W1, byp_W0, byp_W1, bn_weight, bn_bias):
    out = irlin_mx(f64(h2), MS, MG, f64(lin3_W0), f64(lin3_W1))
    out = out + irlin_plain(f64(features), MI0, MI1, f64(byp_W0), f64(byp_W1))
    return batchnorm(out, f64(bn_weight), f64(bn_bias))

@@ -1,0 +1,304 @@
+import math
+from contextlib import ExitStack
+
+import concourse.mybir as mybir
+from concourse.masks import make_identity
+
+BF16 = mybir.dt.bfloat16
+F32 = mybir.dt.float32
+U32 = mybir.dt.uint32
+U8 = mybir.dt.uint8
+FP8X4 = mybir.dt.float8_e4m3fn_x4
+ALU = mybir.AluOpType
+ACT = mybir.ActivationFunctionType
+
+P = 128
+NODES = 128
+DV = 3
+PACK = 4
+HID_S, HID_V = 1024, 512
+IN_S, IN_V = 512, 256
+OUT_S, OUT_V = 512, 256
+S_PASSES = HID_S // (P * PACK)
+S_TILES = OUT_S // P
+V_TILES = OUT_V // P
+EPS = 1e-5
+
+FLOPS = 2 * NODES * (HID_S * OUT_S + DV * HID_V * OUT_V + IN_S * OUT_S + DV * IN_V * OUT_V)
+
+
+def regroup(nc, raw, grouped):
+    nc.vector.tensor_copy(
+        out=grouped.rearrange("p (c i) t -> p c t i", i=4),
+        in_=raw.rearrange("p t (c i) -> p c t i", i=4),
+    )
+
+
+def quantise(nc, grouped, codes, scales):
+    nc.vector.quantize_mx(
+        out=codes.bitcast(FP8X4),
+        scales=scales,
+        in_=grouped.rearrange("p c t -> p (c t)"),
+    )
+
+
+def tile_feedforward_pb_s_kernel(
+    tc, h2, features, lin3_W0, lin3_W1, byp_W0, byp_W1, bn_weight, bn_bias, out
+):
+    nc = tc.nc
+    with ExitStack() as ctx:
+        keep = ctx.enter_context(tc.tile_pool(name="keep", bufs=1))
+        psum = ctx.enter_context(tc.psum_pool(name="psum", bufs=8))
+        ctx.enter_context(tc.manual_schedule())
+
+        W_ROWS = (OUT_S + OUT_V) // P
+        B_ROWS = OUT_S // P
+        prm_rows = keep.tile([P, P], BF16)
+        nc.vector.memset(prm_rows[:], 0.0)
+        nc.scalar.dma_start(out=prm_rows[0:W_ROWS, :], in_=bn_weight.rearrange("(j p) -> j p", p=P))
+        nc.scalar.dma_start(
+            out=prm_rows[W_ROWS : W_ROWS + B_ROWS, :], in_=bn_bias.rearrange("(j p) -> j p", p=P)
+        )
+
+        h2_sb = keep.tile([P, HID_S + DV * HID_V], BF16)
+        nc.sync.dma_start(out=h2_sb[:, HID_S:], in_=h2[:, HID_S:])
+        w1_raw = keep.tile([P, PACK, OUT_V], BF16)
+        nc.sync.dma_start(out=w1_raw[:], in_=lin3_W1.rearrange("(p t) c -> p t c", t=PACK))
+        ft_sb = keep.tile([P, IN_S + DV * IN_V], BF16)
+        nc.sync.dma_start(out=ft_sb[:], in_=features)
+        w0_raw = keep.tile([P, S_PASSES, PACK, OUT_S], BF16)
+        w0_rows = lin3_W0.rearrange("(g p t) c -> g p t c", g=S_PASSES, t=PACK)
+        for g in range(S_PASSES):
+            nc.sync.dma_start(out=w0_raw[:, g], in_=w0_rows[g])
+        nc.sync.dma_start(out=h2_sb[:, :HID_S], in_=h2[:, :HID_S])
+        bw1 = keep.tile([P, IN_V // P, OUT_V], BF16)
+        nc.sync.dma_start(out=bw1[:], in_=byp_W1.rearrange("(t p) c -> p t c", p=P))
+        bw0 = keep.tile([P, IN_S // P, OUT_S], BF16)
+        nc.sync.dma_start(out=bw0[:], in_=byp_W0.rearrange("(t p) c -> p t c", p=P))
+
+        ident_f32 = keep.tile([P, P], F32)
+        nc.vector.memset(ident_f32[:], 0.0)
+        make_identity(nc, ident_f32[:], nomemset=True)
+        ident_bf = keep.tile([P, P], BF16)
+        nc.vector.tensor_copy(out=ident_bf[:], in_=ident_f32[:])
+
+        one = keep.tile([P, 1], F32)
+        nc.vector.memset(one[:], 1.0)
+        table_warm = keep.tile([P, 1], F32)
+        nc.scalar.activation(out=table_warm[:], in_=one[:], func=ACT.Abs_reciprocal_sqrt)
+
+        w0_grouped = keep.tile([P, S_PASSES, OUT_S, PACK], BF16, align_bytes=64)
+        w0_codes = keep.tile([P, S_PASSES, OUT_S], U32, align_bytes=64)
+        w0_scales = keep.tile([P, S_PASSES, OUT_S], U8, align_bytes=64)
+        w1_grouped = keep.tile([P, OUT_V, PACK], BF16, align_bytes=64)
+        w1_codes = keep.tile([P, OUT_V], U32, align_bytes=64)
+        w1_scales = keep.tile([P, OUT_V], U8, align_bytes=64)
+        H_UNITS = S_PASSES + DV
+        h_grouped = keep.tile([P, H_UNITS * NODES * PACK], BF16, align_bytes=64)
+        h_units = h_grouped[:].rearrange("p (a n t) -> p a n t", a=H_UNITS, t=PACK)
+        h_codes = keep.tile([P, H_UNITS, NODES], U32, align_bytes=64)
+        h_scales = keep.tile([P, H_UNITS, NODES], U8, align_bytes=64)
+
+        regroup(nc, w1_raw[:], w1_grouped[:])
+        hv = h2_sb[:, HID_S:].rearrange("n (i d) -> n d i", d=DV)
+        for d in range(DV):
+            a = S_PASSES + d
+            hv_t = psum.tile([P, PACK, NODES], BF16, tag="bank")
+            for t in range(PACK):
+                nc.tensor.transpose(hv_t[:, t, :], hv[:, d, t::PACK], ident_bf[:])
+            nc.scalar.copy(out=h_units[:, a], in_=hv_t[:].rearrange("p t n -> p n t"))
+            quantise(nc, h_units[:, a], h_codes[:, a, :], h_scales[:, a, :])
+            if d == 0:
+                quantise(nc, w1_grouped[:], w1_codes[:], w1_scales[:])
+
+        fv_in = ft_sb[:, IN_S:].rearrange("n (i d) -> n d i", d=DV)
+        fv_t = psum.tile([P, IN_V // P, DV, NODES], BF16, tag="bank")
+        for t in range(IN_V // P):
+            for d in range(DV):
+                nc.tensor.transpose(fv_t[:, t, d, :], fv_in[:, d, P * t : P * (t + 1)], ident_bf[:])
+        fv = keep.tile([P, IN_V // P, DV, NODES], BF16)
+        nc.scalar.copy(out=fv[:], in_=fv_t[:])
+
+        fs_t = psum.tile([P, IN_S // P, NODES], BF16, tag="bank")
+        for t in range(IN_S // P):
+            nc.tensor.transpose(fs_t[:, t, :], ft_sb[:, P * t : P * (t + 1)], ident_bf[:])
+        fs = keep.tile([P, IN_S // P, NODES], BF16)
+        nc.scalar.copy(out=fs[:], in_=fs_t[:])
+
+        prm_t = psum.tile([P, P], BF16, tag="bank")
+        nc.tensor.transpose(prm_t[:], prm_rows[:], ident_bf[:])
+        prm = keep.tile([P, W_ROWS + B_ROWS], F32)
+        nc.scalar.copy(out=prm[:], in_=prm_t[:, : W_ROWS + B_ROWS])
+        weight_s = prm[:, 0:S_TILES]
+        weight_v = prm[:, S_TILES:W_ROWS]
+        bias_s = prm[:, W_ROWS : W_ROWS + B_ROWS]
+
+        for g in range(S_PASSES):
+            regroup(nc, w0_raw[:, g], w0_grouped[:, g])
+        for g in range(S_PASSES):
+            quantise(nc, w0_grouped[:, g], w0_codes[:, g, :], w0_scales[:, g, :])
+
+        mx_v = keep.tile([P, V_TILES, DV, NODES], F32)
+        for c in range(V_TILES):
+            o_cols = slice(P * c, P * (c + 1))
+            acc_v = psum.tile([P, DV, NODES], F32, tag="bank")
+            for d in range(DV):
+                nc.tensor.matmul_mx(
+                    out=acc_v[:, d, :],
+                    lhsT=w1_codes[:, o_cols].bitcast(FP8X4),
+                    lhsT_scale=w1_scales[:, o_cols],
+                    rhs=h_codes[:, S_PASSES + d, :].bitcast(FP8X4),
+                    rhs_scale=h_scales[:, S_PASSES + d, :],
+                    start=True,
+                    stop=True,
+                )
+            nc.scalar.mul(out=mx_v[:, c], in_=acc_v[:], mul=1.0 / math.sqrt(HID_V))
+
+        h2_words = h2_sb[:].bitcast(F32)
+        hs_t = psum.tile([P, S_PASSES, 2, NODES], F32, tag="bank")
+        for g in range(S_PASSES):
+            for u in range(2):
+                words = h2_words[:, 256 * g + u : 256 * (g + 1) : 2]
+                nc.tensor.transpose(hs_t[:, g, u, :], words, ident_f32[:])
+        hs_words = h_grouped[:].bitcast(F32)[:, : S_PASSES * NODES * 2]
+        nc.scalar.copy(
+            out=hs_words.rearrange("p (g n u) -> p g n u", g=S_PASSES, u=2),
+            in_=hs_t[:].rearrange("p g u n -> p g n u"),
+        )
+        for g in range(S_PASSES):
+            quantise(nc, h_units[:, g], h_codes[:, g, :], h_scales[:, g, :])
+
+        y_v = keep.tile([P, V_TILES, DV, NODES], F32)
+        squares = keep.tile([P, V_TILES, DV * NODES], F32)
+        mean_sq = keep.tile([P, V_TILES], F32)
+        byp_v = [
+            psum.tile([P, DV, NODES], F32, tag="bank", name="byp_v%d" % c) for c in range(V_TILES)
+        ]
+        for c in range(V_TILES):
+            for t in range(IN_V // P):
+                nc.tensor.matmul(
+                    out=byp_v[c][:].rearrange("o d n -> o (d n)"),
+                    lhsT=bw1[:, t, P * c : P * (c + 1)],
+                    rhs=fv[:, t].rearrange("p d n -> p (d n)"),
+                    start=(t == 0),
+                    stop=(t == IN_V // P - 1),
+                )
+
+        byp_s = psum.tile([P, S_TILES, NODES], F32, tag="bank")
+        for m in range(S_TILES):
+            for t in range(IN_S // P):
+                nc.tensor.matmul(
+                    out=byp_s[:, m, :],
+                    lhsT=bw0[:, t, P * m : P * (m + 1)],
+                    rhs=fs[:, t, :],
+                    start=(t == 0),
+                    stop=(t == IN_S // P - 1),
+                )
+        bypass_s = keep.tile([P, S_TILES, NODES], F32)
+        nc.scalar.mul(out=bypass_s[:], in_=byp_s[:], mul=1.0 / math.sqrt(IN_S))
+
+        for c in range(V_TILES):
+            nc.vector.scalar_tensor_tensor(
+                out=y_v[:, c],
+                in0=byp_v[c][:],
+                scalar=1.0 / math.sqrt(IN_V),
+                in1=mx_v[:, c],
+                op0=ALU.mult,
+                op1=ALU.add,
+            )
+            nc.scalar.activation(
+                out=squares[:, c, :],
+                in_=y_v[:, c].rearrange("o d n -> o (d n)"),
+                func=ACT.Square,
+                scale=1.0 / math.sqrt(DV * NODES),
+                accum_out=mean_sq[:, c : c + 1],
+            )
+        rstd_v = keep.tile([P, V_TILES], F32)
+        nc.scalar.activation(
+            out=rstd_v[:], in_=mean_sq[:], func=ACT.Abs_reciprocal_sqrt, bias=EPS, scale=1.0
+        )
+
+        y_s = keep.tile([P, S_TILES, NODES], F32)
+        for half in range(2):
+            acc_s = psum.tile([P, 2, NODES], F32, tag="bank")
+            for j in range(2):
+                o_cols = slice(P * (2 * half + j), P * (2 * half + j + 1))
+                for g in range(S_PASSES):
+                    nc.tensor.matmul_mx(
+                        out=acc_s[:, j, :],
+                        lhsT=w0_codes[:, g, o_cols].bitcast(FP8X4),
+                        lhsT_scale=w0_scales[:, g, o_cols],
+                        rhs=h_codes[:, g, :].bitcast(FP8X4),
+                        rhs_scale=h_scales[:, g, :],
+                        start=(g == 0),
+                        stop=(g == S_PASSES - 1),
+                    )
+            nc.vector.scalar_tensor_tensor(
+                out=y_s[:, 2 * half : 2 * half + 2, :],
+                in0=acc_s[:],
+                scalar=1.0 / math.sqrt(HID_S),
+                in1=bypass_s[:, 2 * half : 2 * half + 2, :],
+                op0=ALU.mult,
+                op1=ALU.add,
+            )
+
+        z_v = keep.tile([P, V_TILES, DV, NODES], F32)
+        for c in range(V_TILES):
+            nc.gpsimd.tensor_scalar(
+                out=z_v[:, c],
+                in0=y_v[:, c],
+                scalar1=rstd_v[:, c : c + 1],
+                scalar2=weight_v[:, c : c + 1],
+                op0=ALU.mult,
+                op1=ALU.mult,
+            )
+
+        stats = keep.tile([P, S_TILES, 6], F32)
+        mean_var = keep.tile([P, S_TILES, 2], F32)
+        for m in range(S_TILES):
+            nc.vector.bn_stats(out=stats[:, m, :], in_=y_s[:, m, :])
+        for m in range(S_TILES):
+            nc.vector.bn_aggr(out=mean_var[:, m, :], in_=stats[:, m, :])
+        rstd_s = keep.tile([P, S_TILES], F32)
+        nc.scalar.activation(
+            out=rstd_s[:], in_=mean_var[:, :, 1], func=ACT.Abs_reciprocal_sqrt, bias=EPS, scale=1.0
+        )
+        centred = keep.tile([P, S_TILES, NODES], F32)
+        for m in range(S_TILES):
+            nc.vector.tensor_scalar(
+                out=centred[:, m, :],
+                in0=y_s[:, m, :],
+                scalar1=mean_var[:, m, 0:1],
+                scalar2=weight_s[:, m : m + 1],
+                op0=ALU.subtract,
+                op1=ALU.mult,
+            )
+        z_s = keep.tile([P, S_TILES, NODES], F32)
+        for m in range(S_TILES):
+            nc.vector.tensor_scalar(
+                out=z_s[:, m, :],
+                in0=centred[:, m, :],
+                scalar1=rstd_s[:, m : m + 1],
+                scalar2=bias_s[:, m : m + 1],
+                op0=ALU.mult,
+                op1=ALU.add,
+            )
+
+        out_sb = keep.tile([P, OUT_S + DV * OUT_V], F32)
+        for c in range(V_TILES):
+            zv_t = psum.tile([P, DV, P], F32, tag="bank")
+            for d in range(DV):
+                nc.tensor.transpose(zv_t[:, d, :], z_v[:, c, d, :], ident_f32[:])
+            cols = slice(OUT_S + DV * P * c, OUT_S + DV * P * (c + 1))
+            nc.scalar.copy(
+                out=out_sb[:, cols].rearrange("n (o d) -> n o d", d=DV),
+                in_=zv_t[:].rearrange("n d o -> n o d"),
+            )
+            nc.sync.dma_start(out=out[:, cols], in_=out_sb[:, cols])
+        for half in range(2):
+            zs_t = psum.tile([P, 2, P], F32, tag="bank")
+            for j in range(2):
+                nc.tensor.transpose(zs_t[:, j, :], z_s[:, 2 * half + j, :], ident_f32[:])
+            cols = slice(2 * P * half, 2 * P * (half + 1))
+            nc.vector.tensor_copy(out=out_sb[:, cols], in_=zs_t[:].rearrange("n j o -> n (j o)"))
+            nc.sync.dma_start(out=out[:, cols], in_=out_sb[:, cols])

@@ -27,8 +27,8 @@ EPS = 1e-5
 FLOPS = 2 * NODES * (HID_S * OUT_S + DV * HID_V * OUT_V + IN_S * OUT_S + DV * IN_V * OUT_V)
 
 
-def regroup(nc, raw, grouped):
-    nc.vector.tensor_copy(
+def regroup(copy, raw, grouped):
+    copy(
         out=grouped.rearrange("p (c i) t -> p c t i", i=4),
         in_=raw.rearrange("p t (c i) -> p c t i", i=4),
     )
@@ -42,23 +42,19 @@ def quantise(nc, grouped, codes, scales):
     )
 
 
+def copy_words(nc, out, in_):
+    nc.scalar.copy(out=out.bitcast(F32), in_=in_.bitcast(F32))
+
+
 def tile_feedforward_pb_s_kernel(
     tc, h2, features, lin3_W0, lin3_W1, byp_W0, byp_W1, bn_weight, bn_bias, out
 ):
     nc = tc.nc
     with ExitStack() as ctx:
         keep = ctx.enter_context(tc.tile_pool(name="keep", bufs=1))
-        psum = ctx.enter_context(tc.psum_pool(name="psum", bufs=8))
+        psum = ctx.enter_context(tc.psum_pool(name="psum", bufs=7))
+        junk_psum = ctx.enter_context(tc.psum_pool(name="junk_psum", bufs=1))
         ctx.enter_context(tc.manual_schedule())
-
-        W_ROWS = (OUT_S + OUT_V) // P
-        B_ROWS = OUT_S // P
-        prm_rows = keep.tile([P, P], BF16)
-        nc.vector.memset(prm_rows[:], 0.0)
-        nc.scalar.dma_start(out=prm_rows[0:W_ROWS, :], in_=bn_weight.rearrange("(j p) -> j p", p=P))
-        nc.scalar.dma_start(
-            out=prm_rows[W_ROWS : W_ROWS + B_ROWS, :], in_=bn_bias.rearrange("(j p) -> j p", p=P)
-        )
 
         h2_sb = keep.tile([P, HID_S + DV * HID_V], BF16)
         nc.sync.dma_start(out=h2_sb[:, HID_S:], in_=h2[:, HID_S:])
@@ -71,21 +67,31 @@ def tile_feedforward_pb_s_kernel(
         for g in range(S_PASSES):
             nc.sync.dma_start(out=w0_raw[:, g], in_=w0_rows[g])
         nc.sync.dma_start(out=h2_sb[:, :HID_S], in_=h2[:, :HID_S])
-        bw1 = keep.tile([P, IN_V // P, OUT_V], BF16)
-        nc.sync.dma_start(out=bw1[:], in_=byp_W1.rearrange("(t p) c -> p t c", p=P))
-        bw0 = keep.tile([P, IN_S // P, OUT_S], BF16)
-        nc.sync.dma_start(out=bw0[:], in_=byp_W0.rearrange("(t p) c -> p t c", p=P))
+        W_ROWS = (OUT_S + OUT_V) // P
+        B_ROWS = OUT_S // P
+        prm_rows = keep.tile([P, P], BF16)
+        nc.vector.memset(prm_rows[:], 0.0)
+        nc.scalar.dma_start(out=prm_rows[0:W_ROWS, :], in_=bn_weight.rearrange("(j p) -> j p", p=P))
+        nc.scalar.dma_start(
+            out=prm_rows[W_ROWS : W_ROWS + B_ROWS, :], in_=bn_bias.rearrange("(j p) -> j p", p=P)
+        )
+        bw1 = keep.tile([P, 2, OUT_V], BF16)
+        nc.sync.dma_start(out=bw1[:], in_=byp_W1.rearrange("(p t) c -> p t c", t=2))
+        bw0 = keep.tile([P, 2, 2, OUT_S], BF16)
+        bw0_rows = byp_W0.rearrange("(h p t) c -> h p t c", h=2, t=2)
+        for h in range(2):
+            nc.sync.dma_start(out=bw0[:, h], in_=bw0_rows[h])
+
+        one = keep.tile([P, 1], F32)
+        nc.vector.memset(one[:], 1.0)
+        table_warm = keep.tile([P, 1], F32)
+        nc.scalar.activation(out=table_warm[:], in_=one[:], func=ACT.Abs_reciprocal_sqrt)
 
         ident_f32 = keep.tile([P, P], F32)
         nc.vector.memset(ident_f32[:], 0.0)
         make_identity(nc, ident_f32[:], nomemset=True)
         ident_bf = keep.tile([P, P], BF16)
         nc.vector.tensor_copy(out=ident_bf[:], in_=ident_f32[:])
-
-        one = keep.tile([P, 1], F32)
-        nc.vector.memset(one[:], 1.0)
-        table_warm = keep.tile([P, 1], F32)
-        nc.scalar.activation(out=table_warm[:], in_=one[:], func=ACT.Abs_reciprocal_sqrt)
 
         w0_grouped = keep.tile([P, S_PASSES, OUT_S, PACK], BF16, align_bytes=64)
         w0_codes = keep.tile([P, S_PASSES, OUT_S], U32, align_bytes=64)
@@ -99,45 +105,64 @@ def tile_feedforward_pb_s_kernel(
         h_codes = keep.tile([P, H_UNITS, NODES], U32, align_bytes=64)
         h_scales = keep.tile([P, H_UNITS, NODES], U8, align_bytes=64)
 
-        regroup(nc, w1_raw[:], w1_grouped[:])
+        def quantise_h(nc, first, last):
+            nc.vector.quantize_mx(
+                out=h_codes[:, first:last, :].rearrange("p a n -> p (a n)").bitcast(FP8X4),
+                scales=h_scales[:, first:last, :].rearrange("p a n -> p (a n)"),
+                in_=h_grouped[:, first * NODES * PACK : last * NODES * PACK],
+            )
+
+        junk = junk_psum.tile([P, OUT_V], F32)
+
+        def keep_warm(nc, passes):
+            for i in range(passes):
+                nc.tensor.matmul_mx(
+                    out=junk[:],
+                    lhsT=w1_codes[:, :P].bitcast(FP8X4),
+                    lhsT_scale=w1_scales[:, :P],
+                    rhs=w1_codes[:].bitcast(FP8X4),
+                    rhs_scale=w1_scales[:],
+                    start=True,
+                    stop=True,
+                )
+
         hv = h2_sb[:, HID_S:].rearrange("n (i d) -> n d i", d=DV)
+        h_words = h_grouped[:].bitcast(F32)
         for d in range(DV):
-            a = S_PASSES + d
             hv_t = psum.tile([P, PACK, NODES], BF16, tag="bank")
             for t in range(PACK):
                 nc.tensor.transpose(hv_t[:, t, :], hv[:, d, t::PACK], ident_bf[:])
-            nc.scalar.copy(out=h_units[:, a], in_=hv_t[:].rearrange("p t n -> p n t"))
-            quantise(nc, h_units[:, a], h_codes[:, a, :], h_scales[:, a, :])
-            if d == 0:
-                quantise(nc, w1_grouped[:], w1_codes[:], w1_scales[:])
+            nc.scalar.copy(out=h_units[:, S_PASSES + d], in_=hv_t[:].rearrange("p t n -> p n t"))
+        regroup(nc.vector.tensor_copy, w1_raw[:], w1_grouped[:])
+        quantise(nc, w1_grouped[:], w1_codes[:], w1_scales[:])
+        quantise_h(nc, S_PASSES, S_PASSES + 2)
 
         fv_in = ft_sb[:, IN_S:].rearrange("n (i d) -> n d i", d=DV)
-        fv_t = psum.tile([P, IN_V // P, DV, NODES], BF16, tag="bank")
-        for t in range(IN_V // P):
+        fv_t = psum.tile([P, 2, DV, NODES], BF16, tag="bank")
+        for t in range(2):
             for d in range(DV):
-                nc.tensor.transpose(fv_t[:, t, d, :], fv_in[:, d, P * t : P * (t + 1)], ident_bf[:])
-        fv = keep.tile([P, IN_V // P, DV, NODES], BF16)
-        nc.scalar.copy(out=fv[:], in_=fv_t[:])
+                nc.tensor.transpose(fv_t[:, t, d, :], fv_in[:, d, t::2], ident_bf[:])
+        fv = keep.tile([P, 2, DV, NODES], BF16)
+        copy_words(nc, fv[:].rearrange("p t d n -> p (t d n)"), fv_t[:].rearrange("p t d n -> p (t d n)"))
 
-        fs_t = psum.tile([P, IN_S // P, NODES], BF16, tag="bank")
-        for t in range(IN_S // P):
-            nc.tensor.transpose(fs_t[:, t, :], ft_sb[:, P * t : P * (t + 1)], ident_bf[:])
-        fs = keep.tile([P, IN_S // P, NODES], BF16)
-        nc.scalar.copy(out=fs[:], in_=fs_t[:])
-
-        prm_t = psum.tile([P, P], BF16, tag="bank")
-        nc.tensor.transpose(prm_t[:], prm_rows[:], ident_bf[:])
-        prm = keep.tile([P, W_ROWS + B_ROWS], F32)
-        nc.scalar.copy(out=prm[:], in_=prm_t[:, : W_ROWS + B_ROWS])
-        weight_s = prm[:, 0:S_TILES]
-        weight_v = prm[:, S_TILES:W_ROWS]
-        bias_s = prm[:, W_ROWS : W_ROWS + B_ROWS]
-
+        V_COLS = OUT_S * 3 // 4
         for g in range(S_PASSES):
-            regroup(nc, w0_raw[:, g], w0_grouped[:, g])
-        for g in range(S_PASSES):
-            quantise(nc, w0_grouped[:, g], w0_codes[:, g, :], w0_scales[:, g, :])
+            regroup(nc.vector.tensor_copy, w0_raw[:, g, :, :V_COLS], w0_grouped[:, g, :V_COLS])
+            regroup(nc.scalar.copy, w0_raw[:, g, :, V_COLS:], w0_grouped[:, g, V_COLS:])
+            if g == 0:
+                fs_t = psum.tile([P, 2, 2, NODES], BF16, tag="bank")
+                for h in range(2):
+                    for t in range(2):
+                        nc.tensor.transpose(
+                            fs_t[:, h, t, :], ft_sb[:, 256 * h + t : 256 * (h + 1) : 2], ident_bf[:]
+                        )
+                fs = keep.tile([P, 2, 2, NODES], BF16)
+                copy_words(
+                    nc, fs[:].rearrange("p h t n -> p (h t n)"), fs_t[:].rearrange("p h t n -> p (h t n)")
+                )
+                quantise_h(nc, S_PASSES + 2, S_PASSES + 3)
 
+        keep_warm(nc, 4)
         mx_v = keep.tile([P, V_TILES, DV, NODES], F32)
         for c in range(V_TILES):
             o_cols = slice(P * c, P * (c + 1))
@@ -160,52 +185,62 @@ def tile_feedforward_pb_s_kernel(
             for u in range(2):
                 words = h2_words[:, 256 * g + u : 256 * (g + 1) : 2]
                 nc.tensor.transpose(hs_t[:, g, u, :], words, ident_f32[:])
-        hs_words = h_grouped[:].bitcast(F32)[:, : S_PASSES * NODES * 2]
         nc.scalar.copy(
-            out=hs_words.rearrange("p (g n u) -> p g n u", g=S_PASSES, u=2),
+            out=h_words[:, : S_PASSES * NODES * 2].rearrange("p (g n u) -> p g n u", g=S_PASSES, u=2),
             in_=hs_t[:].rearrange("p g u n -> p g n u"),
         )
         for g in range(S_PASSES):
-            quantise(nc, h_units[:, g], h_codes[:, g, :], h_scales[:, g, :])
+            quantise(nc, w0_grouped[:, g], w0_codes[:, g, :], w0_scales[:, g, :])
+        quantise_h(nc, 0, S_PASSES)
+
+        prm_t = psum.tile([P, P], BF16, tag="bank")
+        nc.tensor.transpose(prm_t[:], prm_rows[:], ident_bf[:])
+        prm = keep.tile([P, W_ROWS + B_ROWS], F32)
+        nc.scalar.copy(out=prm[:], in_=prm_t[:, : W_ROWS + B_ROWS])
+        weight_s = prm[:, 0:S_TILES]
+        weight_v = prm[:, S_TILES:W_ROWS]
+        bias_s = prm[:, W_ROWS : W_ROWS + B_ROWS]
+        keep_warm(nc, 2)
 
         y_v = keep.tile([P, V_TILES, DV, NODES], F32)
-        squares = keep.tile([P, V_TILES, DV * NODES], F32)
-        mean_sq = keep.tile([P, V_TILES], F32)
-        byp_v = [
-            psum.tile([P, DV, NODES], F32, tag="bank", name="byp_v%d" % c) for c in range(V_TILES)
-        ]
         for c in range(V_TILES):
-            for t in range(IN_V // P):
+            byp_v = psum.tile([P, DV, NODES], F32, tag="bank")
+            for t in range(2):
                 nc.tensor.matmul(
-                    out=byp_v[c][:].rearrange("o d n -> o (d n)"),
+                    out=byp_v[:].rearrange("o d n -> o (d n)"),
                     lhsT=bw1[:, t, P * c : P * (c + 1)],
                     rhs=fv[:, t].rearrange("p d n -> p (d n)"),
                     start=(t == 0),
-                    stop=(t == IN_V // P - 1),
+                    stop=(t == 1),
                 )
-
-        byp_s = psum.tile([P, S_TILES, NODES], F32, tag="bank")
-        for m in range(S_TILES):
-            for t in range(IN_S // P):
-                nc.tensor.matmul(
-                    out=byp_s[:, m, :],
-                    lhsT=bw0[:, t, P * m : P * (m + 1)],
-                    rhs=fs[:, t, :],
-                    start=(t == 0),
-                    stop=(t == IN_S // P - 1),
-                )
-        bypass_s = keep.tile([P, S_TILES, NODES], F32)
-        nc.scalar.mul(out=bypass_s[:], in_=byp_s[:], mul=1.0 / math.sqrt(IN_S))
-
-        for c in range(V_TILES):
             nc.vector.scalar_tensor_tensor(
                 out=y_v[:, c],
-                in0=byp_v[c][:],
+                in0=byp_v[:],
                 scalar=1.0 / math.sqrt(IN_V),
                 in1=mx_v[:, c],
                 op0=ALU.mult,
                 op1=ALU.add,
             )
+
+        byp_s = [
+            psum.tile([P, NODES], F32, tag="bank", name="byp_s%d" % m) for m in range(S_TILES)
+        ]
+
+        def bypass_half(h):
+            for m in range(S_TILES):
+                for t in range(2):
+                    nc.tensor.matmul(
+                        out=byp_s[m][:],
+                        lhsT=bw0[:, h, t, P * m : P * (m + 1)],
+                        rhs=fs[:, h, t, :],
+                        start=(h == 0 and t == 0),
+                        stop=(h == 1 and t == 1),
+                    )
+
+        squares = keep.tile([P, V_TILES, DV * NODES], F32)
+        mean_sq = keep.tile([P, V_TILES], F32)
+
+        def square_v(c):
             nc.scalar.activation(
                 out=squares[:, c, :],
                 in_=y_v[:, c].rearrange("o d n -> o (d n)"),
@@ -213,16 +248,15 @@ def tile_feedforward_pb_s_kernel(
                 scale=1.0 / math.sqrt(DV * NODES),
                 accum_out=mean_sq[:, c : c + 1],
             )
-        rstd_v = keep.tile([P, V_TILES], F32)
-        nc.scalar.activation(
-            out=rstd_v[:], in_=mean_sq[:], func=ACT.Abs_reciprocal_sqrt, bias=EPS, scale=1.0
-        )
 
-        y_s = keep.tile([P, S_TILES, NODES], F32)
+        bypass_half(0)
+        square_v(0)
+        mx_s = keep.tile([P, S_TILES, NODES], F32)
         for half in range(2):
             acc_s = psum.tile([P, 2, NODES], F32, tag="bank")
             for j in range(2):
-                o_cols = slice(P * (2 * half + j), P * (2 * half + j + 1))
+                m = 2 * half + j
+                o_cols = slice(P * m, P * (m + 1))
                 for g in range(S_PASSES):
                     nc.tensor.matmul_mx(
                         out=acc_s[:, j, :],
@@ -233,18 +267,30 @@ def tile_feedforward_pb_s_kernel(
                         start=(g == 0),
                         stop=(g == S_PASSES - 1),
                     )
+            nc.scalar.mul(
+                out=mx_s[:, 2 * half : 2 * half + 2, :], in_=acc_s[:], mul=1.0 / math.sqrt(HID_S)
+            )
+        bypass_half(1)
+        y_s = keep.tile([P, S_TILES, NODES], F32)
+        for m in range(S_TILES):
             nc.vector.scalar_tensor_tensor(
-                out=y_s[:, 2 * half : 2 * half + 2, :],
-                in0=acc_s[:],
-                scalar=1.0 / math.sqrt(HID_S),
-                in1=bypass_s[:, 2 * half : 2 * half + 2, :],
+                out=y_s[:, m, :],
+                in0=byp_s[m][:],
+                scalar=1.0 / math.sqrt(IN_S),
+                in1=mx_s[:, m, :],
                 op0=ALU.mult,
                 op1=ALU.add,
             )
 
+        square_v(1)
+        rstd_v = keep.tile([P, V_TILES], F32)
+        nc.scalar.activation(
+            out=rstd_v[:], in_=mean_sq[:], func=ACT.Abs_reciprocal_sqrt, bias=EPS, scale=1.0
+        )
         z_v = keep.tile([P, V_TILES, DV, NODES], F32)
-        for c in range(V_TILES):
-            nc.gpsimd.tensor_scalar(
+
+        def norm_v(engine, c):
+            engine.tensor_scalar(
                 out=z_v[:, c],
                 in0=y_v[:, c],
                 scalar1=rstd_v[:, c : c + 1],
@@ -252,6 +298,8 @@ def tile_feedforward_pb_s_kernel(
                 op0=ALU.mult,
                 op1=ALU.mult,
             )
+
+        norm_v(nc.gpsimd, 0)
 
         stats = keep.tile([P, S_TILES, 6], F32)
         mean_var = keep.tile([P, S_TILES, 2], F32)
@@ -263,6 +311,7 @@ def tile_feedforward_pb_s_kernel(
         nc.scalar.activation(
             out=rstd_s[:], in_=mean_var[:, :, 1], func=ACT.Abs_reciprocal_sqrt, bias=EPS, scale=1.0
         )
+        norm_v(nc.vector, 1)
         centred = keep.tile([P, S_TILES, NODES], F32)
         for m in range(S_TILES):
             nc.vector.tensor_scalar(

@@ -52,8 +52,7 @@ def tile_feedforward_pb_s_kernel(
     nc = tc.nc
     with ExitStack() as ctx:
         keep = ctx.enter_context(tc.tile_pool(name="keep", bufs=1))
-        psum = ctx.enter_context(tc.psum_pool(name="psum", bufs=7))
-        junk_psum = ctx.enter_context(tc.psum_pool(name="junk_psum", bufs=1))
+        psum = ctx.enter_context(tc.psum_pool(name="psum", bufs=8))
         ctx.enter_context(tc.manual_schedule())
 
         h2_sb = keep.tile([P, HID_S + DV * HID_V], BF16)
@@ -76,9 +75,9 @@ def tile_feedforward_pb_s_kernel(
             out=prm_rows[W_ROWS : W_ROWS + B_ROWS, :], in_=bn_bias.rearrange("(j p) -> j p", p=P)
         )
         bw1 = keep.tile([P, 2, OUT_V], BF16)
-        nc.sync.dma_start(out=bw1[:], in_=byp_W1.rearrange("(p t) c -> p t c", t=2))
+        nc.sync.dma_start(out=bw1[:], in_=byp_W1.rearrange("(t p) c -> p t c", t=2))
         bw0 = keep.tile([P, 2, 2, OUT_S], BF16)
-        bw0_rows = byp_W0.rearrange("(h p t) c -> h p t c", h=2, t=2)
+        bw0_rows = byp_W0.rearrange("(h t p) c -> h p t c", h=2, t=2)
         for h in range(2):
             nc.sync.dma_start(out=bw0[:, h], in_=bw0_rows[h])
 
@@ -101,7 +100,6 @@ def tile_feedforward_pb_s_kernel(
         w1_scales = keep.tile([P, OUT_V], U8, align_bytes=64)
         H_UNITS = S_PASSES + DV
         h_grouped = keep.tile([P, H_UNITS * NODES * PACK], BF16, align_bytes=64)
-        h_units = h_grouped[:].rearrange("p (a n t) -> p a n t", a=H_UNITS, t=PACK)
         h_codes = keep.tile([P, H_UNITS, NODES], U32, align_bytes=64)
         h_scales = keep.tile([P, H_UNITS, NODES], U8, align_bytes=64)
 
@@ -112,27 +110,24 @@ def tile_feedforward_pb_s_kernel(
                 in_=h_grouped[:, first * NODES * PACK : last * NODES * PACK],
             )
 
-        junk = junk_psum.tile([P, OUT_V], F32)
-
-        def keep_warm(nc, passes):
-            for i in range(passes):
-                nc.tensor.matmul_mx(
-                    out=junk[:],
-                    lhsT=w1_codes[:, :P].bitcast(FP8X4),
-                    lhsT_scale=w1_scales[:, :P],
-                    rhs=w1_codes[:].bitcast(FP8X4),
-                    rhs_scale=w1_scales[:],
-                    start=True,
-                    stop=True,
-                )
-
-        hv = h2_sb[:, HID_S:].rearrange("n (i d) -> n d i", d=DV)
-        h_words = h_grouped[:].bitcast(F32)
+        hv_in = h2_sb[:, HID_S:].rearrange("n (p u e d) -> n d p u e", u=2, e=2, d=DV)
+        hv = keep.tile([P, DV, 2, P, 2], BF16)
         for d in range(DV):
-            hv_t = psum.tile([P, PACK, NODES], BF16, tag="bank")
-            for t in range(PACK):
-                nc.tensor.transpose(hv_t[:, t, :], hv[:, d, t::PACK], ident_bf[:])
-            nc.scalar.copy(out=h_units[:, S_PASSES + d], in_=hv_t[:].rearrange("p t n -> p n t"))
+            copy = nc.scalar.copy if d == DV - 1 else nc.vector.tensor_copy
+            copy(out=hv[:, d].rearrange("n u p e -> n p u e"), in_=hv_in[:, d])
+        hv_words = hv[:].rearrange("n d u p e -> n (d u p e)").bitcast(F32)
+        h_words = h_grouped[:].bitcast(F32)
+        for ds in ((0, 1), (2,)):
+            hv_t = psum.tile([P, len(ds), 2, NODES], F32, tag="bank")
+            for j, d in enumerate(ds):
+                for u in range(2):
+                    first = P * (2 * d + u)
+                    nc.tensor.transpose(hv_t[:, j, u, :], hv_words[:, first : first + P], ident_f32[:])
+            cols = slice(2 * NODES * (S_PASSES + ds[0]), 2 * NODES * (S_PASSES + ds[-1] + 1))
+            nc.scalar.copy(
+                out=h_words[:, cols].rearrange("p (d n u) -> p d n u", n=NODES, u=2),
+                in_=hv_t[:].rearrange("p d u n -> p d n u"),
+            )
         regroup(nc.vector.tensor_copy, w1_raw[:], w1_grouped[:])
         quantise(nc, w1_grouped[:], w1_codes[:], w1_scales[:])
         quantise_h(nc, S_PASSES, S_PASSES + 2)
@@ -141,7 +136,7 @@ def tile_feedforward_pb_s_kernel(
         fv_t = psum.tile([P, 2, DV, NODES], BF16, tag="bank")
         for t in range(2):
             for d in range(DV):
-                nc.tensor.transpose(fv_t[:, t, d, :], fv_in[:, d, t::2], ident_bf[:])
+                nc.tensor.transpose(fv_t[:, t, d, :], fv_in[:, d, P * t : P * (t + 1)], ident_bf[:])
         fv = keep.tile([P, 2, DV, NODES], BF16)
         copy_words(nc, fv[:].rearrange("p t d n -> p (t d n)"), fv_t[:].rearrange("p t d n -> p (t d n)"))
 
@@ -153,16 +148,14 @@ def tile_feedforward_pb_s_kernel(
                 fs_t = psum.tile([P, 2, 2, NODES], BF16, tag="bank")
                 for h in range(2):
                     for t in range(2):
-                        nc.tensor.transpose(
-                            fs_t[:, h, t, :], ft_sb[:, 256 * h + t : 256 * (h + 1) : 2], ident_bf[:]
-                        )
+                        first = P * (2 * h + t)
+                        nc.tensor.transpose(fs_t[:, h, t, :], ft_sb[:, first : first + P], ident_bf[:])
                 fs = keep.tile([P, 2, 2, NODES], BF16)
                 copy_words(
                     nc, fs[:].rearrange("p h t n -> p (h t n)"), fs_t[:].rearrange("p h t n -> p (h t n)")
                 )
                 quantise_h(nc, S_PASSES + 2, S_PASSES + 3)
 
-        keep_warm(nc, 4)
         mx_v = keep.tile([P, V_TILES, DV, NODES], F32)
         for c in range(V_TILES):
             o_cols = slice(P * c, P * (c + 1))
@@ -200,7 +193,6 @@ def tile_feedforward_pb_s_kernel(
         weight_s = prm[:, 0:S_TILES]
         weight_v = prm[:, S_TILES:W_ROWS]
         bias_s = prm[:, W_ROWS : W_ROWS + B_ROWS]
-        keep_warm(nc, 2)
 
         y_v = keep.tile([P, V_TILES, DV, NODES], F32)
         for c in range(V_TILES):

@@ -55,6 +55,8 @@ def tile_feedforward_pb_s_kernel(
         psum = ctx.enter_context(tc.psum_pool(name="psum", bufs=8))
         ctx.enter_context(tc.manual_schedule())
 
+        one = keep.tile([P, 1], F32)
+        nc.vector.memset(one[:], 1.0)
         h2_sb = keep.tile([P, HID_S + DV * HID_V], BF16)
         nc.sync.dma_start(out=h2_sb[:, HID_S:], in_=h2[:, HID_S:])
         w1_raw = keep.tile([P, PACK, OUT_V], BF16)
@@ -63,26 +65,26 @@ def tile_feedforward_pb_s_kernel(
         nc.sync.dma_start(out=ft_sb[:], in_=features)
         w0_raw = keep.tile([P, S_PASSES, PACK, OUT_S], BF16)
         w0_rows = lin3_W0.rearrange("(g p t) c -> g p t c", g=S_PASSES, t=PACK)
-        for g in range(S_PASSES):
-            nc.sync.dma_start(out=w0_raw[:, g], in_=w0_rows[g])
+        nc.sync.dma_start(out=w0_raw[:, 0], in_=w0_rows[0])
         nc.sync.dma_start(out=h2_sb[:, :HID_S], in_=h2[:, :HID_S])
+        nc.sync.dma_start(out=w0_raw[:, 1], in_=w0_rows[1])
+        bw1 = keep.tile([P, 2, OUT_V], BF16)
+        nc.sync.dma_start(out=bw1[:], in_=byp_W1.rearrange("(t p) c -> p t c", t=2))
+        bw0 = keep.tile([P, 2, 2, OUT_S], BF16)
+        bw0_rows = byp_W0.rearrange("(h p t) c -> h p t c", h=2, t=2)
+        for h in range(2):
+            nc.sync.dma_start(out=bw0[:, h], in_=bw0_rows[h])
         W_ROWS = (OUT_S + OUT_V) // P
         B_ROWS = OUT_S // P
         prm_rows = keep.tile([P, P], BF16)
         nc.vector.memset(prm_rows[:], 0.0)
-        nc.scalar.dma_start(out=prm_rows[0:W_ROWS, :], in_=bn_weight.rearrange("(j p) -> j p", p=P))
-        nc.scalar.dma_start(
+        weight_rows = bn_weight.rearrange("(j p) -> j p", p=P)
+        nc.sync.dma_start(out=prm_rows[0:S_TILES, :], in_=weight_rows[0:S_TILES])
+        nc.sync.dma_start(out=prm_rows[S_TILES:W_ROWS, :], in_=weight_rows[S_TILES:W_ROWS])
+        nc.sync.dma_start(
             out=prm_rows[W_ROWS : W_ROWS + B_ROWS, :], in_=bn_bias.rearrange("(j p) -> j p", p=P)
         )
-        bw1 = keep.tile([P, 2, OUT_V], BF16)
-        nc.sync.dma_start(out=bw1[:], in_=byp_W1.rearrange("(t p) c -> p t c", t=2))
-        bw0 = keep.tile([P, 2, 2, OUT_S], BF16)
-        bw0_rows = byp_W0.rearrange("(h t p) c -> h p t c", h=2, t=2)
-        for h in range(2):
-            nc.sync.dma_start(out=bw0[:, h], in_=bw0_rows[h])
 
-        one = keep.tile([P, 1], F32)
-        nc.vector.memset(one[:], 1.0)
         table_warm = keep.tile([P, 1], F32)
         nc.scalar.activation(out=table_warm[:], in_=one[:], func=ACT.Abs_reciprocal_sqrt)
 
@@ -140,21 +142,38 @@ def tile_feedforward_pb_s_kernel(
         fv = keep.tile([P, 2, DV, NODES], BF16)
         copy_words(nc, fv[:].rearrange("p t d n -> p (t d n)"), fv_t[:].rearrange("p t d n -> p (t d n)"))
 
+        fs_t = psum.tile([P, 2, 2, NODES], BF16, tag="bank")
+        for h in range(2):
+            for t in range(2):
+                nc.tensor.transpose(
+                    fs_t[:, h, t, :], ft_sb[:, 256 * h + t : 256 * (h + 1) : 2], ident_bf[:]
+                )
+        fs = keep.tile([P, 2, 2, NODES], BF16)
+        copy_words(nc, fs[:].rearrange("p h t n -> p (h t n)"), fs_t[:].rearrange("p h t n -> p (h t n)"))
+
         V_COLS = OUT_S * 3 // 4
-        for g in range(S_PASSES):
+
+        def regroup_w0(g):
             regroup(nc.vector.tensor_copy, w0_raw[:, g, :, :V_COLS], w0_grouped[:, g, :V_COLS])
             regroup(nc.scalar.copy, w0_raw[:, g, :, V_COLS:], w0_grouped[:, g, V_COLS:])
-            if g == 0:
-                fs_t = psum.tile([P, 2, 2, NODES], BF16, tag="bank")
-                for h in range(2):
-                    for t in range(2):
-                        first = P * (2 * h + t)
-                        nc.tensor.transpose(fs_t[:, h, t, :], ft_sb[:, first : first + P], ident_bf[:])
-                fs = keep.tile([P, 2, 2, NODES], BF16)
-                copy_words(
-                    nc, fs[:].rearrange("p h t n -> p (h t n)"), fs_t[:].rearrange("p h t n -> p (h t n)")
-                )
-                quantise_h(nc, S_PASSES + 2, S_PASSES + 3)
+
+        regroup_w0(0)
+        quantise_h(nc, S_PASSES + 2, S_PASSES + 3)
+        quantise(nc, w0_grouped[:, 0], w0_codes[:, 0, :], w0_scales[:, 0, :])
+
+        h2_words = h2_sb[:].bitcast(F32)
+        hs_t = psum.tile([P, S_PASSES, 2, NODES], F32, tag="bank")
+        for g in range(S_PASSES):
+            for u in range(2):
+                words = h2_words[:, 256 * g + u : 256 * (g + 1) : 2]
+                nc.tensor.transpose(hs_t[:, g, u, :], words, ident_f32[:])
+        nc.scalar.copy(
+            out=h_words[:, : S_PASSES * NODES * 2].rearrange("p (g n u) -> p g n u", g=S_PASSES, u=2),
+            in_=hs_t[:].rearrange("p g u n -> p g n u"),
+        )
+        regroup_w0(1)
+        quantise_h(nc, 0, S_PASSES)
+        quantise(nc, w0_grouped[:, 1], w0_codes[:, 1, :], w0_scales[:, 1, :])
 
         mx_v = keep.tile([P, V_TILES, DV, NODES], F32)
         for c in range(V_TILES):
@@ -171,28 +190,6 @@ def tile_feedforward_pb_s_kernel(
                     stop=True,
                 )
             nc.scalar.mul(out=mx_v[:, c], in_=acc_v[:], mul=1.0 / math.sqrt(HID_V))
-
-        h2_words = h2_sb[:].bitcast(F32)
-        hs_t = psum.tile([P, S_PASSES, 2, NODES], F32, tag="bank")
-        for g in range(S_PASSES):
-            for u in range(2):
-                words = h2_words[:, 256 * g + u : 256 * (g + 1) : 2]
-                nc.tensor.transpose(hs_t[:, g, u, :], words, ident_f32[:])
-        nc.scalar.copy(
-            out=h_words[:, : S_PASSES * NODES * 2].rearrange("p (g n u) -> p g n u", g=S_PASSES, u=2),
-            in_=hs_t[:].rearrange("p g u n -> p g n u"),
-        )
-        for g in range(S_PASSES):
-            quantise(nc, w0_grouped[:, g], w0_codes[:, g, :], w0_scales[:, g, :])
-        quantise_h(nc, 0, S_PASSES)
-
-        prm_t = psum.tile([P, P], BF16, tag="bank")
-        nc.tensor.transpose(prm_t[:], prm_rows[:], ident_bf[:])
-        prm = keep.tile([P, W_ROWS + B_ROWS], F32)
-        nc.scalar.copy(out=prm[:], in_=prm_t[:, : W_ROWS + B_ROWS])
-        weight_s = prm[:, 0:S_TILES]
-        weight_v = prm[:, S_TILES:W_ROWS]
-        bias_s = prm[:, W_ROWS : W_ROWS + B_ROWS]
 
         y_v = keep.tile([P, V_TILES, DV, NODES], F32)
         for c in range(V_TILES):
@@ -242,7 +239,6 @@ def tile_feedforward_pb_s_kernel(
             )
 
         bypass_half(0)
-        square_v(0)
         mx_s = keep.tile([P, S_TILES, NODES], F32)
         for half in range(2):
             acc_s = psum.tile([P, 2, NODES], F32, tag="bank")
@@ -274,11 +270,32 @@ def tile_feedforward_pb_s_kernel(
                 op1=ALU.add,
             )
 
-        square_v(1)
+        prm_t = psum.tile([P, P], BF16, tag="bank")
+        nc.tensor.transpose(prm_t[:], prm_rows[:], ident_bf[:])
+        junk = psum.tile([P, OUT_V], F32, tag="bank")
+        for i in range(4):
+            nc.tensor.matmul_mx(
+                out=junk[:],
+                lhsT=w1_codes[:, :P].bitcast(FP8X4),
+                lhsT_scale=w1_scales[:, :P],
+                rhs=w1_codes[:].bitcast(FP8X4),
+                rhs_scale=w1_scales[:],
+                start=True,
+                stop=True,
+            )
+
+        for c in range(V_TILES):
+            square_v(c)
         rstd_v = keep.tile([P, V_TILES], F32)
         nc.scalar.activation(
             out=rstd_v[:], in_=mean_sq[:], func=ACT.Abs_reciprocal_sqrt, bias=EPS, scale=1.0
         )
+        prm = keep.tile([P, W_ROWS + B_ROWS], F32)
+        nc.scalar.copy(out=prm[:], in_=prm_t[:, : W_ROWS + B_ROWS])
+        weight_s = prm[:, 0:S_TILES]
+        weight_v = prm[:, S_TILES:W_ROWS]
+        bias_s = prm[:, W_ROWS : W_ROWS + B_ROWS]
+
         z_v = keep.tile([P, V_TILES, DV, NODES], F32)
 
         def norm_v(engine, c):
@@ -326,7 +343,7 @@ def tile_feedforward_pb_s_kernel(
             )
 
         out_sb = keep.tile([P, OUT_S + DV * OUT_V], F32)
-        for c in range(V_TILES):
+        for c in reversed(range(V_TILES)):
             zv_t = psum.tile([P, DV, P], F32, tag="bank")
             for d in range(DV):
                 nc.tensor.transpose(zv_t[:, d, :], z_v[:, c, d, :], ident_f32[:])

@@ -151,13 +151,11 @@ def tile_feedforward_pb_s_kernel(
         fs = keep.tile([P, 2, 2, NODES], BF16)
         copy_words(nc, fs[:].rearrange("p h t n -> p (h t n)"), fs_t[:].rearrange("p h t n -> p (h t n)"))
 
-        V_COLS = OUT_S * 3 // 4
+        def regroup_w0(g, v_cols):
+            regroup(nc.vector.tensor_copy, w0_raw[:, g, :, :v_cols], w0_grouped[:, g, :v_cols])
+            regroup(nc.scalar.copy, w0_raw[:, g, :, v_cols:], w0_grouped[:, g, v_cols:])
 
-        def regroup_w0(g):
-            regroup(nc.vector.tensor_copy, w0_raw[:, g, :, :V_COLS], w0_grouped[:, g, :V_COLS])
-            regroup(nc.scalar.copy, w0_raw[:, g, :, V_COLS:], w0_grouped[:, g, V_COLS:])
-
-        regroup_w0(0)
+        regroup_w0(0, OUT_S * 6 // 8)
         quantise_h(nc, S_PASSES + 2, S_PASSES + 3)
         quantise(nc, w0_grouped[:, 0], w0_codes[:, 0, :], w0_scales[:, 0, :])
 
@@ -171,7 +169,7 @@ def tile_feedforward_pb_s_kernel(
             out=h_words[:, : S_PASSES * NODES * 2].rearrange("p (g n u) -> p g n u", g=S_PASSES, u=2),
             in_=hs_t[:].rearrange("p g u n -> p g n u"),
         )
-        regroup_w0(1)
+        regroup_w0(1, OUT_S * 5 // 8)
         quantise_h(nc, 0, S_PASSES)
         quantise(nc, w0_grouped[:, 1], w0_codes[:, 1, :], w0_scales[:, 1, :])
 
@@ -272,18 +270,6 @@ def tile_feedforward_pb_s_kernel(
 
         prm_t = psum.tile([P, P], BF16, tag="bank")
         nc.tensor.transpose(prm_t[:], prm_rows[:], ident_bf[:])
-        junk = psum.tile([P, OUT_V], F32, tag="bank")
-        for i in range(4):
-            nc.tensor.matmul_mx(
-                out=junk[:],
-                lhsT=w1_codes[:, :P].bitcast(FP8X4),
-                lhsT_scale=w1_scales[:, :P],
-                rhs=w1_codes[:].bitcast(FP8X4),
-                rhs_scale=w1_scales[:],
-                start=True,
-                stop=True,
-            )
-
         for c in range(V_TILES):
             square_v(c)
         rstd_v = keep.tile([P, V_TILES], F32)

import math
from contextlib import ExitStack

import concourse.mybir as mybir
from concourse.masks import make_identity

BF16 = mybir.dt.bfloat16
F32 = mybir.dt.float32
U32 = mybir.dt.uint32
U8 = mybir.dt.uint8
FP8X4 = mybir.dt.float8_e4m3fn_x4
ALU = mybir.AluOpType
ACT = mybir.ActivationFunctionType

P = 128
NODES = 128
DV = 3
PACK = 4
HID_S, HID_V = 1024, 512
IN_S, IN_V = 512, 256
OUT_S, OUT_V = 512, 256
S_PASSES = HID_S // (P * PACK)
S_TILES = OUT_S // P
V_TILES = OUT_V // P
EPS = 1e-5

FLOPS = 2 * NODES * (HID_S * OUT_S + DV * HID_V * OUT_V + IN_S * OUT_S + DV * IN_V * OUT_V)


def regroup(copy, raw, grouped):
    copy(
        out=grouped.rearrange("p (c i) t -> p c t i", i=4),
        in_=raw.rearrange("p t (c i) -> p c t i", i=4),
    )


def quantise(nc, grouped, codes, scales):
    nc.vector.quantize_mx(
        out=codes.bitcast(FP8X4),
        scales=scales,
        in_=grouped.rearrange("p c t -> p (c t)"),
    )


def copy_words(nc, out, in_):
    nc.scalar.copy(out=out.bitcast(F32), in_=in_.bitcast(F32))


def tile_feedforward_pb_s_kernel(
    tc, h2, features, lin3_W0, lin3_W1, byp_W0, byp_W1, bn_weight, bn_bias, out
):
    nc = tc.nc
    with ExitStack() as ctx:
        keep = ctx.enter_context(tc.tile_pool(name="keep", bufs=1))
        psum = ctx.enter_context(tc.psum_pool(name="psum", bufs=8))
        ctx.enter_context(tc.manual_schedule())

        one = keep.tile([P, 1], F32)
        nc.vector.memset(one[:], 1.0)
        h2_sb = keep.tile([P, HID_S + DV * HID_V], BF16)
        nc.sync.dma_start(out=h2_sb[:, HID_S:], in_=h2[:, HID_S:])
        w1_raw = keep.tile([P, PACK, OUT_V], BF16)
        nc.sync.dma_start(out=w1_raw[:], in_=lin3_W1.rearrange("(p t) c -> p t c", t=PACK))
        ft_sb = keep.tile([P, IN_S + DV * IN_V], BF16)
        nc.sync.dma_start(out=ft_sb[:], in_=features)
        w0_raw = keep.tile([P, S_PASSES, PACK, OUT_S], BF16)
        w0_rows = lin3_W0.rearrange("(g p t) c -> g p t c", g=S_PASSES, t=PACK)
        nc.sync.dma_start(out=w0_raw[:, 0], in_=w0_rows[0])
        nc.sync.dma_start(out=h2_sb[:, :HID_S], in_=h2[:, :HID_S])
        nc.sync.dma_start(out=w0_raw[:, 1], in_=w0_rows[1])
        bw1 = keep.tile([P, 2, OUT_V], BF16)
        nc.sync.dma_start(out=bw1[:], in_=byp_W1.rearrange("(t p) c -> p t c", t=2))
        bw0 = keep.tile([P, 2, 2, OUT_S], BF16)
        bw0_rows = byp_W0.rearrange("(h p t) c -> h p t c", h=2, t=2)
        for h in range(2):
            nc.sync.dma_start(out=bw0[:, h], in_=bw0_rows[h])
        W_ROWS = (OUT_S + OUT_V) // P
        B_ROWS = OUT_S // P
        prm_rows = keep.tile([P, P], BF16)
        nc.vector.memset(prm_rows[:], 0.0)
        weight_rows = bn_weight.rearrange("(j p) -> j p", p=P)
        nc.sync.dma_start(out=prm_rows[0:S_TILES, :], in_=weight_rows[0:S_TILES])
        nc.sync.dma_start(out=prm_rows[S_TILES:W_ROWS, :], in_=weight_rows[S_TILES:W_ROWS])
        nc.sync.dma_start(
            out=prm_rows[W_ROWS : W_ROWS + B_ROWS, :], in_=bn_bias.rearrange("(j p) -> j p", p=P)
        )

        table_warm = keep.tile([P, 1], F32)
        nc.scalar.activation(out=table_warm[:], in_=one[:], func=ACT.Abs_reciprocal_sqrt)

        ident_f32 = keep.tile([P, P], F32)
        nc.vector.memset(ident_f32[:], 0.0)
        make_identity(nc, ident_f32[:], nomemset=True)
        ident_bf = keep.tile([P, P], BF16)
        nc.vector.tensor_copy(out=ident_bf[:], in_=ident_f32[:])

        w0_grouped = keep.tile([P, S_PASSES, OUT_S, PACK], BF16, align_bytes=64)
        w0_codes = keep.tile([P, S_PASSES, OUT_S], U32, align_bytes=64)
        w0_scales = keep.tile([P, S_PASSES, OUT_S], U8, align_bytes=64)
        w1_grouped = keep.tile([P, OUT_V, PACK], BF16, align_bytes=64)
        w1_codes = keep.tile([P, OUT_V], U32, align_bytes=64)
        w1_scales = keep.tile([P, OUT_V], U8, align_bytes=64)
        H_UNITS = S_PASSES + DV
        h_grouped = keep.tile([P, H_UNITS * NODES * PACK], BF16, align_bytes=64)
        h_codes = keep.tile([P, H_UNITS, NODES], U32, align_bytes=64)
        h_scales = keep.tile([P, H_UNITS, NODES], U8, align_bytes=64)

        def quantise_h(nc, first, last):
            nc.vector.quantize_mx(
                out=h_codes[:, first:last, :].rearrange("p a n -> p (a n)").bitcast(FP8X4),
                scales=h_scales[:, first:last, :].rearrange("p a n -> p (a n)"),
                in_=h_grouped[:, first * NODES * PACK : last * NODES * PACK],
            )

        hv_in = h2_sb[:, HID_S:].rearrange("n (p u e d) -> n d p u e", u=2, e=2, d=DV)
        hv = keep.tile([P, DV, 2, P, 2], BF16)
        for d in range(DV):
            copy = nc.scalar.copy if d == DV - 1 else nc.vector.tensor_copy
            copy(out=hv[:, d].rearrange("n u p e -> n p u e"), in_=hv_in[:, d])
        hv_words = hv[:].rearrange("n d u p e -> n (d u p e)").bitcast(F32)
        h_words = h_grouped[:].bitcast(F32)
        for ds in ((0, 1), (2,)):
            hv_t = psum.tile([P, len(ds), 2, NODES], F32, tag="bank")
            for j, d in enumerate(ds):
                for u in range(2):
                    first = P * (2 * d + u)
                    nc.tensor.transpose(hv_t[:, j, u, :], hv_words[:, first : first + P], ident_f32[:])
            cols = slice(2 * NODES * (S_PASSES + ds[0]), 2 * NODES * (S_PASSES + ds[-1] + 1))
            nc.scalar.copy(
                out=h_words[:, cols].rearrange("p (d n u) -> p d n u", n=NODES, u=2),
                in_=hv_t[:].rearrange("p d u n -> p d n u"),
            )
        regroup(nc.vector.tensor_copy, w1_raw[:], w1_grouped[:])
        quantise(nc, w1_grouped[:], w1_codes[:], w1_scales[:])
        quantise_h(nc, S_PASSES, S_PASSES + 2)

        fv_in = ft_sb[:, IN_S:].rearrange("n (i d) -> n d i", d=DV)
        fv_t = psum.tile([P, 2, DV, NODES], BF16, tag="bank")
        for t in range(2):
            for d in range(DV):
                nc.tensor.transpose(fv_t[:, t, d, :], fv_in[:, d, P * t : P * (t + 1)], ident_bf[:])
        fv = keep.tile([P, 2, DV, NODES], BF16)
        copy_words(nc, fv[:].rearrange("p t d n -> p (t d n)"), fv_t[:].rearrange("p t d n -> p (t d n)"))

        fs_t = psum.tile([P, 2, 2, NODES], BF16, tag="bank")
        for h in range(2):
            for t in range(2):
                nc.tensor.transpose(
                    fs_t[:, h, t, :], ft_sb[:, 256 * h + t : 256 * (h + 1) : 2], ident_bf[:]
                )
        fs = keep.tile([P, 2, 2, NODES], BF16)
        copy_words(nc, fs[:].rearrange("p h t n -> p (h t n)"), fs_t[:].rearrange("p h t n -> p (h t n)"))

        def regroup_w0(g, v_cols):
            regroup(nc.vector.tensor_copy, w0_raw[:, g, :, :v_cols], w0_grouped[:, g, :v_cols])
            regroup(nc.scalar.copy, w0_raw[:, g, :, v_cols:], w0_grouped[:, g, v_cols:])

        regroup_w0(0, OUT_S * 6 // 8)
        quantise_h(nc, S_PASSES + 2, S_PASSES + 3)
        quantise(nc, w0_grouped[:, 0], w0_codes[:, 0, :], w0_scales[:, 0, :])

        h2_words = h2_sb[:].bitcast(F32)
        hs_t = psum.tile([P, S_PASSES, 2, NODES], F32, tag="bank")
        for g in range(S_PASSES):
            for u in range(2):
                words = h2_words[:, 256 * g + u : 256 * (g + 1) : 2]
                nc.tensor.transpose(hs_t[:, g, u, :], words, ident_f32[:])
        nc.scalar.copy(
            out=h_words[:, : S_PASSES * NODES * 2].rearrange("p (g n u) -> p g n u", g=S_PASSES, u=2),
            in_=hs_t[:].rearrange("p g u n -> p g n u"),
        )
        regroup_w0(1, OUT_S * 5 // 8)
        quantise_h(nc, 0, S_PASSES)
        quantise(nc, w0_grouped[:, 1], w0_codes[:, 1, :], w0_scales[:, 1, :])

        mx_v = keep.tile([P, V_TILES, DV, NODES], F32)
        for c in range(V_TILES):
            o_cols = slice(P * c, P * (c + 1))
            acc_v = psum.tile([P, DV, NODES], F32, tag="bank")
            for d in range(DV):
                nc.tensor.matmul_mx(
                    out=acc_v[:, d, :],
                    lhsT=w1_codes[:, o_cols].bitcast(FP8X4),
                    lhsT_scale=w1_scales[:, o_cols],
                    rhs=h_codes[:, S_PASSES + d, :].bitcast(FP8X4),
                    rhs_scale=h_scales[:, S_PASSES + d, :],
                    start=True,
                    stop=True,
                )
            nc.scalar.mul(out=mx_v[:, c], in_=acc_v[:], mul=1.0 / math.sqrt(HID_V))

        y_v = keep.tile([P, V_TILES, DV, NODES], F32)
        for c in range(V_TILES):
            byp_v = psum.tile([P, DV, NODES], F32, tag="bank")
            for t in range(2):
                nc.tensor.matmul(
                    out=byp_v[:].rearrange("o d n -> o (d n)"),
                    lhsT=bw1[:, t, P * c : P * (c + 1)],
                    rhs=fv[:, t].rearrange("p d n -> p (d n)"),
                    start=(t == 0),
                    stop=(t == 1),
                )
            nc.vector.scalar_tensor_tensor(
                out=y_v[:, c],
                in0=byp_v[:],
                scalar=1.0 / math.sqrt(IN_V),
                in1=mx_v[:, c],
                op0=ALU.mult,
                op1=ALU.add,
            )

        byp_s = [
            psum.tile([P, NODES], F32, tag="bank", name="byp_s%d" % m) for m in range(S_TILES)
        ]

        def bypass_half(h):
            for m in range(S_TILES):
                for t in range(2):
                    nc.tensor.matmul(
                        out=byp_s[m][:],
                        lhsT=bw0[:, h, t, P * m : P * (m + 1)],
                        rhs=fs[:, h, t, :],
                        start=(h == 0 and t == 0),
                        stop=(h == 1 and t == 1),
                    )

        squares = keep.tile([P, V_TILES, DV * NODES], F32)
        mean_sq = keep.tile([P, V_TILES], F32)

        def square_v(c):
            nc.scalar.activation(
                out=squares[:, c, :],
                in_=y_v[:, c].rearrange("o d n -> o (d n)"),
                func=ACT.Square,
                scale=1.0 / math.sqrt(DV * NODES),
                accum_out=mean_sq[:, c : c + 1],
            )

        bypass_half(0)
        mx_s = keep.tile([P, S_TILES, NODES], F32)
        for half in range(2):
            acc_s = psum.tile([P, 2, NODES], F32, tag="bank")
            for j in range(2):
                m = 2 * half + j
                o_cols = slice(P * m, P * (m + 1))
                for g in range(S_PASSES):
                    nc.tensor.matmul_mx(
                        out=acc_s[:, j, :],
                        lhsT=w0_codes[:, g, o_cols].bitcast(FP8X4),
                        lhsT_scale=w0_scales[:, g, o_cols],
                        rhs=h_codes[:, g, :].bitcast(FP8X4),
                        rhs_scale=h_scales[:, g, :],
                        start=(g == 0),
                        stop=(g == S_PASSES - 1),
                    )
            nc.scalar.mul(
                out=mx_s[:, 2 * half : 2 * half + 2, :], in_=acc_s[:], mul=1.0 / math.sqrt(HID_S)
            )
        bypass_half(1)
        y_s = keep.tile([P, S_TILES, NODES], F32)
        for m in range(S_TILES):
            nc.vector.scalar_tensor_tensor(
                out=y_s[:, m, :],
                in0=byp_s[m][:],
                scalar=1.0 / math.sqrt(IN_S),
                in1=mx_s[:, m, :],
                op0=ALU.mult,
                op1=ALU.add,
            )

        prm_t = psum.tile([P, P], BF16, tag="bank")
        nc.tensor.transpose(prm_t[:], prm_rows[:], ident_bf[:])
        for c in range(V_TILES):
            square_v(c)
        rstd_v = keep.tile([P, V_TILES], F32)
        nc.scalar.activation(
            out=rstd_v[:], in_=mean_sq[:], func=ACT.Abs_reciprocal_sqrt, bias=EPS, scale=1.0
        )
        prm = keep.tile([P, W_ROWS + B_ROWS], F32)
        nc.scalar.copy(out=prm[:], in_=prm_t[:, : W_ROWS + B_ROWS])
        weight_s = prm[:, 0:S_TILES]
        weight_v = prm[:, S_TILES:W_ROWS]
        bias_s = prm[:, W_ROWS : W_ROWS + B_ROWS]

        z_v = keep.tile([P, V_TILES, DV, NODES], F32)

        def norm_v(engine, c):
            engine.tensor_scalar(
                out=z_v[:, c],
                in0=y_v[:, c],
                scalar1=rstd_v[:, c : c + 1],
                scalar2=weight_v[:, c : c + 1],
                op0=ALU.mult,
                op1=ALU.mult,
            )

        norm_v(nc.gpsimd, 0)

        stats = keep.tile([P, S_TILES, 6], F32)
        mean_var = keep.tile([P, S_TILES, 2], F32)
        for m in range(S_TILES):
            nc.vector.bn_stats(out=stats[:, m, :], in_=y_s[:, m, :])
        for m in range(S_TILES):
            nc.vector.bn_aggr(out=mean_var[:, m, :], in_=stats[:, m, :])
        rstd_s = keep.tile([P, S_TILES], F32)
        nc.scalar.activation(
            out=rstd_s[:], in_=mean_var[:, :, 1], func=ACT.Abs_reciprocal_sqrt, bias=EPS, scale=1.0
        )
        norm_v(nc.vector, 1)
        centred = keep.tile([P, S_TILES, NODES], F32)
        for m in range(S_TILES):
            nc.vector.tensor_scalar(
                out=centred[:, m, :],
                in0=y_s[:, m, :],
                scalar1=mean_var[:, m, 0:1],
                scalar2=weight_s[:, m : m + 1],
                op0=ALU.subtract,
                op1=ALU.mult,
            )
        z_s = keep.tile([P, S_TILES, NODES], F32)
        for m in range(S_TILES):
            nc.vector.tensor_scalar(
                out=z_s[:, m, :],
                in0=centred[:, m, :],
                scalar1=rstd_s[:, m : m + 1],
                scalar2=bias_s[:, m : m + 1],
                op0=ALU.mult,
                op1=ALU.add,
            )

        out_sb = keep.tile([P, OUT_S + DV * OUT_V], F32)
        for c in reversed(range(V_TILES)):
            zv_t = psum.tile([P, DV, P], F32, tag="bank")
            for d in range(DV):
                nc.tensor.transpose(zv_t[:, d, :], z_v[:, c, d, :], ident_f32[:])
            cols = slice(OUT_S + DV * P * c, OUT_S + DV * P * (c + 1))
            nc.scalar.copy(
                out=out_sb[:, cols].rearrange("n (o d) -> n o d", d=DV),
                in_=zv_t[:].rearrange("n d o -> n o d"),
            )
            nc.sync.dma_start(out=out[:, cols], in_=out_sb[:, cols])
        for half in range(2):
            zs_t = psum.tile([P, 2, P], F32, tag="bank")
            for j in range(2):
                nc.tensor.transpose(zs_t[:, j, :], z_s[:, 2 * half + j, :], ident_f32[:])
            cols = slice(2 * P * half, 2 * P * (half + 1))
            nc.vector.tensor_copy(out=out_sb[:, cols], in_=zs_t[:].rearrange("n j o -> n (j o)"))
            nc.sync.dma_start(out=out[:, cols], in_=out_sb[:, cols])
